import numpy as np
import ml_dtypes


def mxq(x, axis, fmt="e4m3"):
    dtype, down = {"e4m3": (ml_dtypes.float8_e4m3fn, 7), "e5m2": (ml_dtypes.float8_e5m2, 14)}[fmt]
    v = np.moveaxis(np.asarray(x, np.float32).astype(ml_dtypes.bfloat16).astype(np.float64), axis, -1)
    blocks = v.reshape(v.shape[:-1] + (-1, 32))
    amax = np.abs(blocks).max(-1, keepdims=True)
    byte = np.maximum(np.where(amax > 0, np.frexp(amax)[1] - 1 + 127, 0) - down, 1)
    scale = np.exp2(byte - 127.0)
    codes = (blocks / scale).astype(np.float32).astype(dtype).astype(np.float64)
    return np.moveaxis((codes * scale).reshape(v.shape), -1, axis)


WIDE = False


def mx_kscale(k):
    if not WIDE:
        return np.ones(k)
    levels = np.array([10, -10, 5, -5, 0])
    a = np.random.permutation(np.resize(levels, k // 512 * 4)).reshape(k // 512, 4)
    idx = np.arange(k)
    return np.exp2(a[idx // 512, idx % 128 // 32])


BF16 = ml_dtypes.bfloat16


def bf(x):
    return np.asarray(x, np.float32).astype(BF16)


def f64(x):
    return np.asarray(x).astype(np.float64)


E2M1 = np.array([0.0, 0.5, 1.0, 1.5, 2.0, 3.0, 4.0, 6.0, -0.0, -0.5, -1.0, -1.5, -2.0, -3.0, -4.0, -6.0])


def pack_weight(w, fmt):
    k, n = w.shape
    w = f64(bf(w)).reshape(k // 32, 32, n)
    amax = np.abs(w).max(1)
    if fmt == "e4m3":
        byte = np.frexp(amax)[1] - 1 + 127 - 7
    else:
        mant, ex = np.frexp(amax / 6.0)
        byte = np.where(mant > 0.5, ex, ex - 1) + 127
    byte = np.clip(np.where(amax > 0, byte, 1), 1, 254)
    scaled = (w * np.exp2(127.0 - byte)[:, None, :]).reshape(k, n).astype(np.float32)
    by_word = np.ascontiguousarray(scaled.reshape(k // 512, 128, 4, n).transpose(0, 1, 3, 2))
    if fmt == "e4m3":
        words = by_word.astype(ml_dtypes.float8_e4m3fn).view(np.uint8)
    else:
        c = by_word.astype(ml_dtypes.float4_e2m1fn).view(np.uint8) & 0xF
        words = c[..., 0::2] | (c[..., 1::2] << 4)
    return np.ascontiguousarray(words), np.ascontiguousarray(byte.astype(np.uint8).reshape(k // 512, 16, n))


def unpack_weight(words, scales, fmt):
    g, p, n, _ = words.shape
    if fmt == "e4m3":
        vals = np.ascontiguousarray(words).view(ml_dtypes.float8_e4m3fn).astype(np.float64)
    else:
        nib = np.empty((g, p, n, 4), np.uint8)
        nib[..., 0::2] = words & 0xF
        nib[..., 1::2] = words >> 4
        vals = E2M1[nib]
    vals = vals * np.repeat(np.exp2(scales.astype(np.float64) - 127.0), 8, axis=1)[..., None]
    return vals.transpose(0, 1, 3, 2).reshape(g * 512, n)


B, H, L, E, QD = 4, 1, 128, 16384, 128
EPS = 1e-5


def build_decay_mask(num_heads, max_len):
    r = f64(np.arange(max_len))
    dec = np.array([1.0 - 2.0 ** (-5 - h) for h in range(num_heads)])
    expo = r[None, :] - r[:, None]
    return np.where(r[:, None] >= r[None, :], dec[:, None, None] ** expo[None], 0.0)


def setup_inputs():
    s = mx_kscale(E)
    kv = (0.1 + 0.32 * np.random.standard_normal((B, H, L, QD))) * (0.1 + 0.32 * np.random.standard_normal((B, H, L, QD)))
    x = bf(np.random.standard_normal((B, H, L, E)) * s)
    Wq = np.random.standard_normal((QD, E)) / np.sqrt(E) / s
    Wq_words, Wq_scales = pack_weight(np.ascontiguousarray(Wq.T), "e4m3")
    return {"x": x,
            "Wq_words": Wq_words,
            "Wq_scales": Wq_scales,
            "bq": bf(0.3 + 0.3 * np.random.standard_normal(QD)),
            "kv": bf(kv),
            "decay_mask": bf(build_decay_mask(H, L))}


def reference(x, Wq_words, Wq_scales, bq, kv, decay_mask):
    b, h, l, e = x.shape
    Q = (mxq(f64(x), 3, "e4m3") @ unpack_weight(Wq_words, Wq_scales, "e4m3")) + f64(bq)
    D = f64(decay_mask)[0, :l, :l]
    y = Q * (f64(kv) @ D.T)
    mean = y.mean(axis=(2, 3), keepdims=True)
    var = ((y - mean) ** 2).mean(axis=(2, 3), keepdims=True)
    y = (y - mean) / np.sqrt(var + EPS)
    return y.reshape(b, l, -1)

@@ -1,0 +1,241 @@
+from contextlib import ExitStack
+
+import concourse.mybir as mybir
+from concourse.masks import make_identity
+
+F32 = mybir.dt.float32
+BF16 = mybir.dt.bfloat16
+I32 = mybir.dt.int32
+U32 = mybir.dt.uint32
+U8 = mybir.dt.uint8
+FP8X4 = mybir.dt.float8_e4m3fn_x4
+ALU = mybir.AluOpType
+ACT = mybir.ActivationFunctionType
+
+P = 128
+SAMPLES = 4
+TOKENS = 128
+FEATURES = 128
+K_TOTAL = 16384
+EPS = 1e-5
+
+PACK = 4
+K_PASS = P * PACK
+PASSES = K_TOTAL // K_PASS
+PAIRS = 2
+WORDS_PER_PASS = P * PAIRS
+
+BANK_PASSES = 2
+UNIT_PASSES = 8
+UNIT_BANKS = UNIT_PASSES // BANK_PASSES
+UNIT_K = UNIT_PASSES * K_PASS
+UNITS_PER_SAMPLE = PASSES // UNIT_PASSES
+UNITS = SAMPLES * UNITS_PER_SAMPLE
+HALF_PASSES = UNIT_PASSES // 2
+HALF_COLS = HALF_PASSES * TOKENS
+
+SCALE_ROWS = 4
+QUADRANTS = 4
+
+FLOPS = 2 * SAMPLES * TOKENS * FEATURES * (K_TOTAL + P)
+
+
+def tile_parallelretention_pb_k_kernel(tc, x, Wq_words, Wq_scales, bq, kv, decay_mask, out):
+    nc = tc.nc
+    with ExitStack() as ctx:
+        const = ctx.enter_context(tc.tile_pool(name="const", bufs=1))
+        x_pool = ctx.enter_context(tc.tile_pool(name="x", bufs=UNITS))
+        grouped_pool = ctx.enter_context(tc.tile_pool(name="grouped", bufs=2))
+        codes_pool = ctx.enter_context(tc.tile_pool(name="codes", bufs=3))
+        norm_pool = ctx.enter_context(tc.tile_pool(name="norm", bufs=2))
+        psum_xt = ctx.enter_context(tc.psum_pool(name="psum_xt", bufs=5))
+        psum_q = ctx.enter_context(tc.psum_pool(name="psum_q", bufs=1))
+        psum_norm = ctx.enter_context(tc.psum_pool(name="psum_norm", bufs=1))
+        ctx.enter_context(tc.manual_schedule())
+
+        ident_f32 = const.tile([P, P], F32)
+        make_identity(nc, ident_f32[:])
+        ident_bf16 = const.tile([P, P], BF16)
+        make_identity(nc, ident_bf16[:])
+        mean_weights = const.tile([P, P], F32)
+        nc.gpsimd.memset(mean_weights[:], 1.0 / (TOKENS * FEATURES))
+
+        w_codes = const.tile([P, PASSES, FEATURES], U32, align_bytes=64)
+        w_scales = const.tile([P, PASSES, FEATURES], U8, align_bytes=64)
+        nc.vector.memset(w_scales[:].bitcast(I32), 0)
+        bias_rows = const.tile([P, FEATURES], BF16)
+        nc.vector.memset(bias_rows[:].bitcast(I32), 0)
+
+        kv_sb = const.tile([P, SAMPLES, P], BF16)
+        nc.scalar.dma_start(out=kv_sb[:], in_=kv.rearrange("b o l k -> l (b o) k"))
+        d_sb = const.tile([P, P], BF16)
+        nc.scalar.dma_start(out=d_sb[:], in_=decay_mask[0])
+        nc.scalar.dma_start(out=bias_rows[0:1, :], in_=bq.unsqueeze(0))
+
+        x_tiles = []
+        for i in range(UNITS):
+            b, c = divmod(i, UNITS_PER_SAMPLE)
+            x_t = x_pool.tile([P, UNIT_K], BF16)
+            nc.sync.dma_start(out=x_t[:], in_=x[b, 0, :, c * UNIT_K : (c + 1) * UNIT_K])
+            x_tiles.append(x_t)
+            if i == 0:
+                for quadrant in range(QUADRANTS):
+                    rows = slice(SCALE_ROWS * quadrant, SCALE_ROWS * (quadrant + 1))
+                    nc.sync.dma_start(
+                        out=w_scales[32 * quadrant : 32 * quadrant + SCALE_ROWS].bitcast(I32),
+                        in_=Wq_scales[:, rows, :].rearrange("g r n -> r g n").bitcast(I32),
+                    )
+            if b == 0:
+                passes = slice(c * UNIT_PASSES, (c + 1) * UNIT_PASSES)
+                nc.sync.dma_start(
+                    out=w_codes[:, passes, :].bitcast(I32),
+                    in_=Wq_words[passes].rearrange("g p n t -> p g (n t)").bitcast(I32),
+                )
+
+        one = const.tile([P, 1], F32)
+        nc.vector.memset(one[:], 1.0)
+        warm = const.tile([P, 1], F32)
+        nc.scalar.activation(out=warm[:], in_=one[:], func=ACT.Sqrt)
+
+        small_ps = psum_xt.tile([P, SAMPLES + 2, P], BF16, tag="xt")
+        for b in range(SAMPLES):
+            nc.tensor.transpose(small_ps[:, b, :], kv_sb[:, b, :], ident_bf16[:])
+        nc.tensor.transpose(small_ps[:, SAMPLES, :], d_sb[:], ident_bf16[:])
+        nc.tensor.transpose(small_ps[:, SAMPLES + 1, :], bias_rows[:], ident_bf16[:])
+        kvT_dT = const.tile([P, SAMPLES + 1, P], BF16)
+        nc.vector.tensor_copy(out=kvT_dT[:], in_=small_ps[:, 0 : SAMPLES + 1, :])
+        bias_col = const.tile([P, 1], F32)
+        nc.vector.tensor_copy(out=bias_col[:], in_=small_ps[:, SAMPLES + 1, 0:1])
+        gT_ps = psum_xt.tile([P, SAMPLES * TOKENS], F32, tag="xt")
+        nc.tensor.matmul(
+            out=gT_ps[:],
+            lhsT=kvT_dT[:, SAMPLES, :],
+            rhs=kvT_dT[:, 0:SAMPLES, :].rearrange("k b l -> k (b l)"),
+            start=True,
+            stop=True,
+        )
+        gT = const.tile([P, SAMPLES * TOKENS], F32)
+        nc.scalar.copy(out=gT[:], in_=gT_ps[:])
+
+        x_codes = {}
+        x_scales = {}
+        qT = {}
+        norm = {}
+
+        def transpose_and_quantise(i):
+            x_words = x_tiles[i][:].bitcast(F32)
+            grouped = grouped_pool.tile([P, UNIT_PASSES * TOKENS * PACK], BF16, align_bytes=64)
+            grouped_words = grouped[:].bitcast(F32).rearrange("p (g r u) -> p g r u", g=UNIT_PASSES, u=PAIRS)
+            codes = codes_pool.tile([P, UNIT_PASSES * TOKENS], U32, align_bytes=64)
+            scales = codes_pool.tile([P, UNIT_PASSES * TOKENS], U8, align_bytes=64)
+            x_codes[i] = codes
+            x_scales[i] = scales
+            for j in range(UNIT_BANKS):
+                xt_ps = psum_xt.tile([P, BANK_PASSES, PAIRS, TOKENS], F32, tag="xt")
+                for g in range(BANK_PASSES):
+                    first = (j * BANK_PASSES + g) * WORDS_PER_PASS
+                    for u in range(PAIRS):
+                        nc.tensor.transpose(
+                            xt_ps[:, g, u, :],
+                            x_words[:, first + u : first + WORDS_PER_PASS : PAIRS],
+                            ident_f32[:],
+                        )
+                empty_bank = nc.vector.tensor_copy if j == UNIT_BANKS - 1 else nc.scalar.copy
+                empty_bank(
+                    out=grouped_words[:, j * BANK_PASSES : (j + 1) * BANK_PASSES, :, :],
+                    in_=xt_ps[:].rearrange("p g u r -> p g r u"),
+                )
+                if j % 2 == 1:
+                    half = j // 2
+                    cols = slice(half * HALF_COLS, (half + 1) * HALF_COLS)
+                    nc.vector.quantize_mx(
+                        out=codes[:, cols].bitcast(FP8X4),
+                        scales=scales[:, cols],
+                        in_=grouped[:, half * HALF_COLS * PACK : (half + 1) * HALF_COLS * PACK],
+                    )
+
+        def multiply(i):
+            b, c = divmod(i, UNITS_PER_SAMPLE)
+            if c == 0:
+                qT_ps = psum_q.tile([P, TOKENS], F32)
+                qT[b] = qT_ps
+            for g in range(UNIT_PASSES):
+                w_pass = c * UNIT_PASSES + g
+                cols = slice(g * TOKENS, (g + 1) * TOKENS)
+                nc.tensor.matmul_mx(
+                    out=qT[b][:],
+                    lhsT=w_codes[:, w_pass, :].bitcast(FP8X4),
+                    lhsT_scale=w_scales[:, w_pass, :],
+                    rhs=x_codes[i][:, cols].bitcast(FP8X4),
+                    rhs_scale=x_scales[i][:, cols],
+                    start=(w_pass == 0),
+                    stop=(w_pass == PASSES - 1),
+                )
+
+        def product(b):
+            yT = norm_pool.tile([P, TOKENS], F32)
+            row_sum = norm_pool.tile([P, 1], F32)
+            nc.vector.scalar_tensor_tensor(
+                out=yT[:],
+                in0=qT[b][:],
+                scalar=bias_col[:, 0:1],
+                in1=gT[:, b * TOKENS : (b + 1) * TOKENS],
+                op0=ALU.add,
+                op1=ALU.mult,
+                accum_out=row_sum[:],
+            )
+            norm[b, "yT"] = yT
+            norm[b, "row_sum"] = row_sum
+
+        def centre(b):
+            mean_ps = psum_norm.tile([P, 1], F32)
+            nc.tensor.matmul(out=mean_ps[:], lhsT=mean_weights[:], rhs=norm[b, "row_sum"][:], start=True, stop=True)
+            y_ps = psum_norm.tile([P, FEATURES], F32)
+            nc.tensor.transpose(y_ps[:], norm[b, "yT"][:], ident_f32[:])
+            neg_mean = norm_pool.tile([P, 1], F32)
+            nc.vector.tensor_scalar_mul(out=neg_mean[:], in0=mean_ps[:], scalar1=-1.0)
+            squares = norm_pool.tile([P, TOKENS], F32)
+            row_squares = norm_pool.tile([P, 1], F32)
+            nc.scalar.activation(
+                out=squares[:],
+                in_=norm[b, "yT"][:],
+                func=ACT.Square,
+                bias=neg_mean[:, 0:1],
+                accum_out=row_squares[:],
+            )
+            norm[b, "y_ps"] = y_ps
+            norm[b, "neg_mean"] = neg_mean
+            norm[b, "row_squares"] = row_squares
+
+        def scale_and_store(b):
+            var_ps = psum_norm.tile([P, 1], F32, tag="mean_ps")
+            nc.tensor.matmul(out=var_ps[:], lhsT=mean_weights[:], rhs=norm[b, "row_squares"][:], start=True, stop=True)
+            std = norm_pool.tile([P, 1], F32)
+            nc.scalar.activation(out=std[:], in_=var_ps[:], func=ACT.Sqrt, bias=EPS)
+            rstd = norm_pool.tile([P, 1], F32)
+            nc.vector.reciprocal(out=rstd[:], in_=std[:])
+            result = norm_pool.tile([P, FEATURES], F32)
+            nc.vector.tensor_scalar(
+                out=result[:],
+                in0=norm[b, "y_ps"][:],
+                scalar1=norm[b, "neg_mean"][:, 0:1],
+                scalar2=rstd[:, 0:1],
+                op0=ALU.add,
+                op1=ALU.mult,
+            )
+            nc.sync.dma_start(out=out[b], in_=result[:])
+
+        def sample_that_ended(i):
+            return i // UNITS_PER_SAMPLE if 0 <= i < UNITS and i % UNITS_PER_SAMPLE == UNITS_PER_SAMPLE - 1 else None
+
+        for i in range(UNITS + 3):
+            if i < UNITS:
+                transpose_and_quantise(i)
+            if sample_that_ended(i - 3) is not None:
+                scale_and_store(sample_that_ended(i - 3))
+            if sample_that_ended(i - 2) is not None:
+                centre(sample_that_ended(i - 2))
+            if 1 <= i <= UNITS:
+                multiply(i - 1)
+            if sample_that_ended(i - 1) is not None:
+                product(sample_that_ended(i - 1))

@@ -33,6 +33,7 @@ UNITS_PER_SAMPLE = PASSES // UNIT_PASSES
 UNITS = SAMPLES * UNITS_PER_SAMPLE
 HALF_PASSES = UNIT_PASSES // 2
 HALF_COLS = HALF_PASSES * TOKENS
+HALF_WORDS = HALF_PASSES * WORDS_PER_PASS
 
 SCALE_ROWS = 4
 QUADRANTS = 4
@@ -45,6 +46,7 @@ def tile_parallelretention_pb_k_kernel(tc, x, Wq_words, Wq_scales, bq, kv, decay
     with ExitStack() as ctx:
         const = ctx.enter_context(tc.tile_pool(name="const", bufs=1))
         x_pool = ctx.enter_context(tc.tile_pool(name="x", bufs=UNITS))
+        sorted_pool = ctx.enter_context(tc.tile_pool(name="sorted", bufs=4))
         grouped_pool = ctx.enter_context(tc.tile_pool(name="grouped", bufs=2))
         codes_pool = ctx.enter_context(tc.tile_pool(name="codes", bufs=3))
         norm_pool = ctx.enter_context(tc.tile_pool(name="norm", bufs=2))
@@ -117,13 +119,24 @@ def tile_parallelretention_pb_k_kernel(tc, x, Wq_words, Wq_scales, bq, kv, decay
         gT = const.tile([P, SAMPLES * TOKENS], F32)
         nc.scalar.copy(out=gT[:], in_=gT_ps[:])
 
+        x_sorted = {}
         x_codes = {}
         x_scales = {}
         qT = {}
         norm = {}
 
-        def transpose_and_quantise(i):
+        def sort_words(i, half):
             x_words = x_tiles[i][:].bitcast(F32)
+            sorted_words = sorted_pool.tile([P, HALF_PASSES, PAIRS, P], F32)
+            nc.vector.tensor_copy(
+                out=sorted_words[:],
+                in_=x_words[:, half * HALF_WORDS : (half + 1) * HALF_WORDS].rearrange(
+                    "r (g p u) -> r g u p", g=HALF_PASSES, u=PAIRS
+                ),
+            )
+            x_sorted[i, half] = sorted_words
+
+        def transpose_and_quantise(i):
             grouped = grouped_pool.tile([P, UNIT_PASSES * TOKENS * PACK], BF16, align_bytes=64)
             grouped_words = grouped[:].bitcast(F32).rearrange("p (g r u) -> p g r u", g=UNIT_PASSES, u=PAIRS)
             codes = codes_pool.tile([P, UNIT_PASSES * TOKENS], U32, align_bytes=64)
@@ -131,22 +144,22 @@ def tile_parallelretention_pb_k_kernel(tc, x, Wq_words, Wq_scales, bq, kv, decay
             x_codes[i] = codes
             x_scales[i] = scales
             for j in range(UNIT_BANKS):
+                half = j // 2
+                if j % 2 == 0 and i + 1 < UNITS:
+                    sort_words(i + 1, half)
                 xt_ps = psum_xt.tile([P, BANK_PASSES, PAIRS, TOKENS], F32, tag="xt")
                 for g in range(BANK_PASSES):
-                    first = (j * BANK_PASSES + g) * WORDS_PER_PASS
                     for u in range(PAIRS):
                         nc.tensor.transpose(
                             xt_ps[:, g, u, :],
-                            x_words[:, first + u : first + WORDS_PER_PASS : PAIRS],
+                            x_sorted[i, half][:, (j % 2) * BANK_PASSES + g, u, :],
                             ident_f32[:],
                         )
-                empty_bank = nc.vector.tensor_copy if j == UNIT_BANKS - 1 else nc.scalar.copy
-                empty_bank(
+                nc.scalar.copy(
                     out=grouped_words[:, j * BANK_PASSES : (j + 1) * BANK_PASSES, :, :],
                     in_=xt_ps[:].rearrange("p g u r -> p g r u"),
                 )
                 if j % 2 == 1:
-                    half = j // 2
                     cols = slice(half * HALF_COLS, (half + 1) * HALF_COLS)
                     nc.vector.quantize_mx(
                         out=codes[:, cols].bitcast(FP8X4),
@@ -228,6 +241,8 @@ def tile_parallelretention_pb_k_kernel(tc, x, Wq_words, Wq_scales, bq, kv, decay
         def sample_that_ended(i):
             return i // UNITS_PER_SAMPLE if 0 <= i < UNITS and i % UNITS_PER_SAMPLE == UNITS_PER_SAMPLE - 1 else None
 
+        sort_words(0, 0)
+        sort_words(0, 1)
         for i in range(UNITS + 3):
             if i < UNITS:
                 transpose_and_quantise(i)

@@ -48,7 +48,7 @@ def tile_parallelretention_pb_k_kernel(tc, x, Wq_words, Wq_scales, bq, kv, decay
         x_pool = ctx.enter_context(tc.tile_pool(name="x", bufs=UNITS))
         sorted_pool = ctx.enter_context(tc.tile_pool(name="sorted", bufs=4))
         grouped_pool = ctx.enter_context(tc.tile_pool(name="grouped", bufs=2))
-        codes_pool = ctx.enter_context(tc.tile_pool(name="codes", bufs=3))
+        codes_pool = ctx.enter_context(tc.tile_pool(name="codes", bufs=4))
         norm_pool = ctx.enter_context(tc.tile_pool(name="norm", bufs=2))
         psum_xt = ctx.enter_context(tc.psum_pool(name="psum_xt", bufs=5))
         psum_q = ctx.enter_context(tc.psum_pool(name="psum_q", bufs=1))
@@ -243,14 +243,14 @@ def tile_parallelretention_pb_k_kernel(tc, x, Wq_words, Wq_scales, bq, kv, decay
 
         sort_words(0, 0)
         sort_words(0, 1)
-        for i in range(UNITS + 3):
+        for i in range(UNITS + 4):
             if i < UNITS:
                 transpose_and_quantise(i)
+            if sample_that_ended(i - 4) is not None:
+                scale_and_store(sample_that_ended(i - 4))
             if sample_that_ended(i - 3) is not None:
-                scale_and_store(sample_that_ended(i - 3))
+                centre(sample_that_ended(i - 3))
+            if 2 <= i <= UNITS + 1:
+                multiply(i - 2)
             if sample_that_ended(i - 2) is not None:
-                centre(sample_that_ended(i - 2))
-            if 1 <= i <= UNITS:
-                multiply(i - 1)
-            if sample_that_ended(i - 1) is not None:
-                product(sample_that_ended(i - 1))
+                product(sample_that_ended(i - 2))

@@ -136,6 +136,11 @@ def tile_parallelretention_pb_k_kernel(tc, x, Wq_words, Wq_scales, bq, kv, decay
             )
             x_sorted[i, half] = sorted_words
 
+        def words_of_pass(i, g, u):
+            if g < HALF_PASSES:
+                return x_sorted[i, 0][:, g, u, :]
+            return x_tiles[i][:].bitcast(F32)[:, g * WORDS_PER_PASS + u : (g + 1) * WORDS_PER_PASS : PAIRS]
+
         def transpose_and_quantise(i):
             grouped = grouped_pool.tile([P, UNIT_PASSES * TOKENS * PACK], BF16, align_bytes=64)
             grouped_words = grouped[:].bitcast(F32).rearrange("p (g r u) -> p g r u", g=UNIT_PASSES, u=PAIRS)
@@ -145,16 +150,12 @@ def tile_parallelretention_pb_k_kernel(tc, x, Wq_words, Wq_scales, bq, kv, decay
             x_scales[i] = scales
             for j in range(UNIT_BANKS):
                 half = j // 2
-                if j % 2 == 0 and i + 1 < UNITS:
-                    sort_words(i + 1, half)
+                if j == 0 and i + 1 < UNITS:
+                    sort_words(i + 1, 0)
                 xt_ps = psum_xt.tile([P, BANK_PASSES, PAIRS, TOKENS], F32, tag="xt")
                 for g in range(BANK_PASSES):
                     for u in range(PAIRS):
-                        nc.tensor.transpose(
-                            xt_ps[:, g, u, :],
-                            x_sorted[i, half][:, (j % 2) * BANK_PASSES + g, u, :],
-                            ident_f32[:],
-                        )
+                        nc.tensor.transpose(xt_ps[:, g, u, :], words_of_pass(i, j * BANK_PASSES + g, u), ident_f32[:])
                 nc.scalar.copy(
                     out=grouped_words[:, j * BANK_PASSES : (j + 1) * BANK_PASSES, :, :],
                     in_=xt_ps[:].rearrange("p g u r -> p g r u"),
@@ -242,7 +243,6 @@ def tile_parallelretention_pb_k_kernel(tc, x, Wq_words, Wq_scales, bq, kv, decay
             return i // UNITS_PER_SAMPLE if 0 <= i < UNITS and i % UNITS_PER_SAMPLE == UNITS_PER_SAMPLE - 1 else None
 
         sort_words(0, 0)
-        sort_words(0, 1)
         for i in range(UNITS + 4):
             if i < UNITS:
                 transpose_and_quantise(i)

@@ -31,12 +31,14 @@ UNIT_BANKS = UNIT_PASSES // BANK_PASSES
 UNIT_K = UNIT_PASSES * K_PASS
 UNITS_PER_SAMPLE = PASSES // UNIT_PASSES
 UNITS = SAMPLES * UNITS_PER_SAMPLE
-HALF_PASSES = UNIT_PASSES // 2
-HALF_COLS = HALF_PASSES * TOKENS
-HALF_WORDS = HALF_PASSES * WORDS_PER_PASS
+BANK_COLS = BANK_PASSES * TOKENS
+SORTED_PASSES = 4
 
 SCALE_ROWS = 4
 QUADRANTS = 4
+
+MEAN_COL = FEATURES
+VAR_COL = FEATURES + 2
 
 FLOPS = 2 * SAMPLES * TOKENS * FEATURES * (K_TOTAL + P)
 
@@ -45,12 +47,13 @@ def tile_parallelretention_pb_k_kernel(tc, x, Wq_words, Wq_scales, bq, kv, decay
     nc = tc.nc
     with ExitStack() as ctx:
         const = ctx.enter_context(tc.tile_pool(name="const", bufs=1))
-        x_pool = ctx.enter_context(tc.tile_pool(name="x", bufs=UNITS))
-        sorted_pool = ctx.enter_context(tc.tile_pool(name="sorted", bufs=4))
+        x_pool = ctx.enter_context(tc.tile_pool(name="x", bufs=UNITS - 2))
+        x_edge_pool = ctx.enter_context(tc.tile_pool(name="x_edge", bufs=4))
+        sorted_pool = ctx.enter_context(tc.tile_pool(name="sorted", bufs=3))
         grouped_pool = ctx.enter_context(tc.tile_pool(name="grouped", bufs=2))
         codes_pool = ctx.enter_context(tc.tile_pool(name="codes", bufs=4))
         norm_pool = ctx.enter_context(tc.tile_pool(name="norm", bufs=2))
-        psum_xt = ctx.enter_context(tc.psum_pool(name="psum_xt", bufs=5))
+        psum_xt = ctx.enter_context(tc.psum_pool(name="psum_xt", bufs=6))
         psum_q = ctx.enter_context(tc.psum_pool(name="psum_q", bufs=1))
         psum_norm = ctx.enter_context(tc.psum_pool(name="psum_norm", bufs=1))
         ctx.enter_context(tc.manual_schedule())
@@ -67,57 +70,79 @@ def tile_parallelretention_pb_k_kernel(tc, x, Wq_words, Wq_scales, bq, kv, decay
         nc.vector.memset(w_scales[:].bitcast(I32), 0)
         bias_rows = const.tile([P, FEATURES], BF16)
         nc.vector.memset(bias_rows[:].bitcast(I32), 0)
-
         kv_sb = const.tile([P, SAMPLES, P], BF16)
-        nc.scalar.dma_start(out=kv_sb[:], in_=kv.rearrange("b o l k -> l (b o) k"))
         d_sb = const.tile([P, P], BF16)
-        nc.scalar.dma_start(out=d_sb[:], in_=decay_mask[0])
-        nc.scalar.dma_start(out=bias_rows[0:1, :], in_=bq.unsqueeze(0))
 
-        x_tiles = []
-        for i in range(UNITS):
+        def is_edge(i):
+            return i == 0 or i == UNITS - 1
+
+        x_parts = {}
+
+        def load_x(i):
             b, c = divmod(i, UNITS_PER_SAMPLE)
-            x_t = x_pool.tile([P, UNIT_K], BF16)
-            nc.sync.dma_start(out=x_t[:], in_=x[b, 0, :, c * UNIT_K : (c + 1) * UNIT_K])
-            x_tiles.append(x_t)
-            if i == 0:
-                for quadrant in range(QUADRANTS):
-                    rows = slice(SCALE_ROWS * quadrant, SCALE_ROWS * (quadrant + 1))
-                    nc.sync.dma_start(
-                        out=w_scales[32 * quadrant : 32 * quadrant + SCALE_ROWS].bitcast(I32),
-                        in_=Wq_scales[:, rows, :].rearrange("g r n -> r g n").bitcast(I32),
-                    )
-            if b == 0:
-                passes = slice(c * UNIT_PASSES, (c + 1) * UNIT_PASSES)
-                nc.sync.dma_start(
-                    out=w_codes[:, passes, :].bitcast(I32),
-                    in_=Wq_words[passes].rearrange("g p n t -> p g (n t)").bitcast(I32),
-                )
+            parts = 2 if is_edge(i) else 1
+            pool = x_edge_pool if is_edge(i) else x_pool
+            x_parts[i] = []
+            for h in range(parts):
+                width = UNIT_K // parts
+                x_t = pool.tile([P, width], BF16, name="x_t")
+                first = c * UNIT_K + h * width
+                nc.sync.dma_start(out=x_t[:], in_=x[b, 0, :, first : first + width])
+                x_parts[i].append(x_t)
+
+        def load_w(c):
+            passes = slice(c * UNIT_PASSES, (c + 1) * UNIT_PASSES)
+            nc.sync.dma_start(
+                out=w_codes[:, passes, :].bitcast(I32),
+                in_=Wq_words[passes].rearrange("g p n t -> p g (n t)").bitcast(I32),
+            )
+
+        load_x(0)
+        load_x(1)
+        for quadrant in range(QUADRANTS):
+            rows = slice(SCALE_ROWS * quadrant, SCALE_ROWS * (quadrant + 1))
+            nc.sync.dma_start(
+                out=w_scales[32 * quadrant : 32 * quadrant + SCALE_ROWS].bitcast(I32),
+                in_=Wq_scales[:, rows, :].rearrange("g r n -> r g n").bitcast(I32),
+            )
+        for c in range(UNITS_PER_SAMPLE):
+            load_w(c)
+            load_x(c + 2)
+            if c == 1:
+                nc.sync.dma_start(out=kv_sb[:], in_=kv.rearrange("b o l k -> l (b o) k"))
+                nc.sync.dma_start(out=d_sb[:], in_=decay_mask[0])
+                nc.sync.dma_start(out=bias_rows[0:1, :], in_=bq.unsqueeze(0))
+        for i in range(UNITS_PER_SAMPLE + 2, UNITS):
+            load_x(i)
 
         one = const.tile([P, 1], F32)
         nc.vector.memset(one[:], 1.0)
         warm = const.tile([P, 1], F32)
-        nc.scalar.activation(out=warm[:], in_=one[:], func=ACT.Sqrt)
+        nc.scalar.activation(out=warm[:], in_=one[:], func=ACT.Abs_reciprocal_sqrt)
 
-        small_ps = psum_xt.tile([P, SAMPLES + 2, P], BF16, tag="xt")
-        for b in range(SAMPLES):
-            nc.tensor.transpose(small_ps[:, b, :], kv_sb[:, b, :], ident_bf16[:])
-        nc.tensor.transpose(small_ps[:, SAMPLES, :], d_sb[:], ident_bf16[:])
-        nc.tensor.transpose(small_ps[:, SAMPLES + 1, :], bias_rows[:], ident_bf16[:])
         kvT_dT = const.tile([P, SAMPLES + 1, P], BF16)
-        nc.vector.tensor_copy(out=kvT_dT[:], in_=small_ps[:, 0 : SAMPLES + 1, :])
         bias_col = const.tile([P, 1], F32)
-        nc.vector.tensor_copy(out=bias_col[:], in_=small_ps[:, SAMPLES + 1, 0:1])
-        gT_ps = psum_xt.tile([P, SAMPLES * TOKENS], F32, tag="xt")
-        nc.tensor.matmul(
-            out=gT_ps[:],
-            lhsT=kvT_dT[:, SAMPLES, :],
-            rhs=kvT_dT[:, 0:SAMPLES, :].rearrange("k b l -> k (b l)"),
-            start=True,
-            stop=True,
-        )
         gT = const.tile([P, SAMPLES * TOKENS], F32)
-        nc.scalar.copy(out=gT[:], in_=gT_ps[:])
+
+        def transpose_small_inputs():
+            small_ps = psum_xt.tile([P, SAMPLES + 2, P], BF16, tag="xt")
+            for b in range(SAMPLES):
+                nc.tensor.transpose(small_ps[:, b, :], kv_sb[:, b, :], ident_bf16[:])
+            nc.tensor.transpose(small_ps[:, SAMPLES, :], d_sb[:], ident_bf16[:])
+            nc.tensor.transpose(small_ps[:, SAMPLES + 1, :], bias_rows[:], ident_bf16[:])
+            nc.vector.tensor_copy(out=kvT_dT[:], in_=small_ps[:, 0 : SAMPLES + 1, :])
+            nc.vector.tensor_copy(out=bias_col[:], in_=small_ps[:, SAMPLES + 1, 0:1])
+
+        def multiply_g():
+            gT_ps = psum_xt.tile([P, SAMPLES * TOKENS], F32, tag="xt")
+            nc.tensor.matmul(
+                out=gT_ps[:],
+                lhsT=kvT_dT[:, SAMPLES, :],
+                rhs=kvT_dT[:, 0:SAMPLES, :].rearrange("k b l -> k (b l)"),
+                start=True,
+                stop=True,
+            )
+            nc.scalar.copy(out=gT[:], in_=gT_ps[:])
 
         x_sorted = {}
         x_codes = {}
@@ -125,48 +150,62 @@ def tile_parallelretention_pb_k_kernel(tc, x, Wq_words, Wq_scales, bq, kv, decay
         qT = {}
         norm = {}
 
-        def sort_words(i, half):
-            x_words = x_tiles[i][:].bitcast(F32)
-            sorted_words = sorted_pool.tile([P, HALF_PASSES, PAIRS, P], F32)
+        def sort_words(i):
+            x_words = x_parts[i][0][:].bitcast(F32)
+            sorted_words = sorted_pool.tile([P, SORTED_PASSES, PAIRS, P], F32)
             nc.vector.tensor_copy(
                 out=sorted_words[:],
-                in_=x_words[:, half * HALF_WORDS : (half + 1) * HALF_WORDS].rearrange(
-                    "r (g p u) -> r g u p", g=HALF_PASSES, u=PAIRS
+                in_=x_words[:, 0 : SORTED_PASSES * WORDS_PER_PASS].rearrange(
+                    "r (g p u) -> r g u p", g=SORTED_PASSES, u=PAIRS
                 ),
             )
-            x_sorted[i, half] = sorted_words
+            x_sorted[i] = sorted_words
 
         def words_of_pass(i, g, u):
-            if g < HALF_PASSES:
-                return x_sorted[i, 0][:, g, u, :]
-            return x_tiles[i][:].bitcast(F32)[:, g * WORDS_PER_PASS + u : (g + 1) * WORDS_PER_PASS : PAIRS]
+            if i in x_sorted and g < SORTED_PASSES:
+                return x_sorted[i][:, g, u, :]
+            part, g_in_part = divmod(g, UNIT_PASSES // len(x_parts[i]))
+            x_words = x_parts[i][part][:].bitcast(F32)
+            return x_words[:, g_in_part * WORDS_PER_PASS + u : (g_in_part + 1) * WORDS_PER_PASS : PAIRS]
 
         def transpose_and_quantise(i):
+            if i + 1 < UNITS and not is_edge(i + 1):
+                sort_words(i + 1)
             grouped = grouped_pool.tile([P, UNIT_PASSES * TOKENS * PACK], BF16, align_bytes=64)
             grouped_words = grouped[:].bitcast(F32).rearrange("p (g r u) -> p g r u", g=UNIT_PASSES, u=PAIRS)
             codes = codes_pool.tile([P, UNIT_PASSES * TOKENS], U32, align_bytes=64)
             scales = codes_pool.tile([P, UNIT_PASSES * TOKENS], U8, align_bytes=64)
             x_codes[i] = codes
             x_scales[i] = scales
+
+            def quantise(first_bank, banks):
+                cols = slice(first_bank * BANK_COLS, (first_bank + banks) * BANK_COLS)
+                nc.vector.quantize_mx(
+                    out=codes[:, cols].bitcast(FP8X4),
+                    scales=scales[:, cols],
+                    in_=grouped[:, first_bank * BANK_COLS * PACK : (first_bank + banks) * BANK_COLS * PACK],
+                )
+
+            vector_banks = (1, 3) if is_edge(i) else (2,) if i % 2 == 1 else ()
             for j in range(UNIT_BANKS):
-                half = j // 2
-                if j == 0 and i + 1 < UNITS:
-                    sort_words(i + 1, 0)
                 xt_ps = psum_xt.tile([P, BANK_PASSES, PAIRS, TOKENS], F32, tag="xt")
                 for g in range(BANK_PASSES):
                     for u in range(PAIRS):
                         nc.tensor.transpose(xt_ps[:, g, u, :], words_of_pass(i, j * BANK_PASSES + g, u), ident_f32[:])
-                nc.scalar.copy(
+                copy = nc.vector.tensor_copy if j in vector_banks else nc.scalar.copy
+                copy(
                     out=grouped_words[:, j * BANK_PASSES : (j + 1) * BANK_PASSES, :, :],
                     in_=xt_ps[:].rearrange("p g u r -> p g r u"),
                 )
-                if j % 2 == 1:
-                    cols = slice(half * HALF_COLS, (half + 1) * HALF_COLS)
-                    nc.vector.quantize_mx(
-                        out=codes[:, cols].bitcast(FP8X4),
-                        scales=scales[:, cols],
-                        in_=grouped[:, half * HALF_COLS * PACK : (half + 1) * HALF_COLS * PACK],
-                    )
+                if is_edge(i):
+                    if j >= 1:
+                        quantise(j - 1, 1)
+                    if j == UNIT_BANKS - 1:
+                        quantise(j, 1)
+                elif j == 2:
+                    quantise(0, 2)
+                elif j == 3:
+                    quantise(2, 2)
 
         def multiply(i):
             b, c = divmod(i, UNITS_PER_SAMPLE)
@@ -202,39 +241,40 @@ def tile_parallelretention_pb_k_kernel(tc, x, Wq_words, Wq_scales, bq, kv, decay
             norm[b, "row_sum"] = row_sum
 
         def centre(b):
-            mean_ps = psum_norm.tile([P, 1], F32)
-            nc.tensor.matmul(out=mean_ps[:], lhsT=mean_weights[:], rhs=norm[b, "row_sum"][:], start=True, stop=True)
-            y_ps = psum_norm.tile([P, FEATURES], F32)
-            nc.tensor.transpose(y_ps[:], norm[b, "yT"][:], ident_f32[:])
-            neg_mean = norm_pool.tile([P, 1], F32)
-            nc.vector.tensor_scalar_mul(out=neg_mean[:], in0=mean_ps[:], scalar1=-1.0)
-            squares = norm_pool.tile([P, TOKENS], F32)
+            norm_ps = psum_norm.tile([P, FEATURES + 4], F32)
+            mean_ps = norm_ps[:, MEAN_COL : MEAN_COL + 1]
+            nc.tensor.matmul(out=mean_ps, lhsT=mean_weights[:], rhs=norm[b, "row_sum"][:], start=True, stop=True)
+            nc.tensor.transpose(norm_ps[:, 0:FEATURES], norm[b, "yT"][:], ident_f32[:])
+            products = norm_pool.tile([P, TOKENS], F32)
             row_squares = norm_pool.tile([P, 1], F32)
-            nc.scalar.activation(
-                out=squares[:],
-                in_=norm[b, "yT"][:],
-                func=ACT.Square,
-                bias=neg_mean[:, 0:1],
+            nc.vector.scalar_tensor_tensor(
+                out=products[:],
+                in0=norm[b, "yT"][:],
+                scalar=mean_ps,
+                in1=norm[b, "yT"][:],
+                op0=ALU.subtract,
+                op1=ALU.mult,
                 accum_out=row_squares[:],
             )
-            norm[b, "y_ps"] = y_ps
-            norm[b, "neg_mean"] = neg_mean
+            mean = norm_pool.tile([P, 1], F32)
+            nc.vector.tensor_copy(out=mean[:], in_=mean_ps)
+            norm[b, "ps"] = norm_ps
+            norm[b, "mean"] = mean
             norm[b, "row_squares"] = row_squares
 
         def scale_and_store(b):
-            var_ps = psum_norm.tile([P, 1], F32, tag="mean_ps")
-            nc.tensor.matmul(out=var_ps[:], lhsT=mean_weights[:], rhs=norm[b, "row_squares"][:], start=True, stop=True)
-            std = norm_pool.tile([P, 1], F32)
-            nc.scalar.activation(out=std[:], in_=var_ps[:], func=ACT.Sqrt, bias=EPS)
+            norm_ps = norm[b, "ps"]
+            var_ps = norm_ps[:, VAR_COL : VAR_COL + 1]
+            nc.tensor.matmul(out=var_ps, lhsT=mean_weights[:], rhs=norm[b, "row_squares"][:], start=True, stop=True)
             rstd = norm_pool.tile([P, 1], F32)
-            nc.vector.reciprocal(out=rstd[:], in_=std[:])
+            nc.scalar.activation(out=rstd[:], in_=var_ps, func=ACT.Abs_reciprocal_sqrt, bias=EPS)
             result = norm_pool.tile([P, FEATURES], F32)
             nc.vector.tensor_scalar(
                 out=result[:],
-                in0=norm[b, "y_ps"][:],
-                scalar1=norm[b, "neg_mean"][:, 0:1],
+                in0=norm_ps[:, 0:FEATURES],
+                scalar1=norm[b, "mean"][:, 0:1],
                 scalar2=rstd[:, 0:1],
-                op0=ALU.add,
+                op0=ALU.subtract,
                 op1=ALU.mult,
             )
             nc.sync.dma_start(out=out[b], in_=result[:])
@@ -242,15 +282,26 @@ def tile_parallelretention_pb_k_kernel(tc, x, Wq_words, Wq_scales, bq, kv, decay
         def sample_that_ended(i):
             return i // UNITS_PER_SAMPLE if 0 <= i < UNITS and i % UNITS_PER_SAMPLE == UNITS_PER_SAMPLE - 1 else None
 
-        sort_words(0, 0)
-        for i in range(UNITS + 4):
-            if i < UNITS:
-                transpose_and_quantise(i)
+        last = UNITS - 1
+        for i in range(UNITS):
+            if i == last:
+                multiply(i - 2)
+            transpose_and_quantise(i)
+            if i == UNITS_PER_SAMPLE:
+                transpose_small_inputs()
             if sample_that_ended(i - 4) is not None:
                 scale_and_store(sample_that_ended(i - 4))
             if sample_that_ended(i - 3) is not None:
                 centre(sample_that_ended(i - 3))
-            if 2 <= i <= UNITS + 1:
+            if i == last:
+                multiply(i - 1)
+                multiply(i)
+            elif i >= 2:
                 multiply(i - 2)
+            if i == UNITS_PER_SAMPLE:
+                multiply_g()
             if sample_that_ended(i - 2) is not None:
                 product(sample_that_ended(i - 2))
+        product(SAMPLES - 1)
+        centre(SAMPLES - 1)
+        scale_and_store(SAMPLES - 1)

@@ -31,8 +31,14 @@ UNIT_BANKS = UNIT_PASSES // BANK_PASSES
 UNIT_K = UNIT_PASSES * K_PASS
 UNITS_PER_SAMPLE = PASSES // UNIT_PASSES
 UNITS = SAMPLES * UNITS_PER_SAMPLE
+ORDER = [(b, c) for b in range(SAMPLES) for c in range(UNITS_PER_SAMPLE)]
 BANK_COLS = BANK_PASSES * TOKENS
-SORTED_PASSES = 4
+SORTED_PASSES = 6
+
+FIRST_SORTED = UNIT_PASSES - SORTED_PASSES
+
+W_AFTER = (1, 2, 3, 4)
+G_LOAD = 3
 
 SCALE_ROWS = 4
 QUADRANTS = 4
@@ -50,12 +56,11 @@ def tile_parallelretention_pb_k_kernel(tc, x, Wq_words, Wq_scales, bq, kv, decay
         x_pool = ctx.enter_context(tc.tile_pool(name="x", bufs=UNITS - 2))
         x_edge_pool = ctx.enter_context(tc.tile_pool(name="x_edge", bufs=4))
         sorted_pool = ctx.enter_context(tc.tile_pool(name="sorted", bufs=3))
-        grouped_pool = ctx.enter_context(tc.tile_pool(name="grouped", bufs=2))
+        grouped_pool = ctx.enter_context(tc.tile_pool(name="grouped", bufs=3))
         codes_pool = ctx.enter_context(tc.tile_pool(name="codes", bufs=4))
         norm_pool = ctx.enter_context(tc.tile_pool(name="norm", bufs=2))
         psum_xt = ctx.enter_context(tc.psum_pool(name="psum_xt", bufs=6))
-        psum_q = ctx.enter_context(tc.psum_pool(name="psum_q", bufs=1))
-        psum_norm = ctx.enter_context(tc.psum_pool(name="psum_norm", bufs=1))
+        psum_q = ctx.enter_context(tc.psum_pool(name="psum_q", bufs=2))
         ctx.enter_context(tc.manual_schedule())
 
         ident_f32 = const.tile([P, P], F32)
@@ -79,7 +84,7 @@ def tile_parallelretention_pb_k_kernel(tc, x, Wq_words, Wq_scales, bq, kv, decay
         x_parts = {}
 
         def load_x(i):
-            b, c = divmod(i, UNITS_PER_SAMPLE)
+            b, c = ORDER[i]
             parts = 2 if is_edge(i) else 1
             pool = x_edge_pool if is_edge(i) else x_pool
             x_parts[i] = []
@@ -97,23 +102,21 @@ def tile_parallelretention_pb_k_kernel(tc, x, Wq_words, Wq_scales, bq, kv, decay
                 in_=Wq_words[passes].rearrange("g p n t -> p g (n t)").bitcast(I32),
             )
 
-        load_x(0)
-        load_x(1)
-        for quadrant in range(QUADRANTS):
-            rows = slice(SCALE_ROWS * quadrant, SCALE_ROWS * (quadrant + 1))
-            nc.sync.dma_start(
-                out=w_scales[32 * quadrant : 32 * quadrant + SCALE_ROWS].bitcast(I32),
-                in_=Wq_scales[:, rows, :].rearrange("g r n -> r g n").bitcast(I32),
-            )
-        for c in range(UNITS_PER_SAMPLE):
-            load_w(c)
-            load_x(c + 2)
-            if c == 1:
+        for i in range(UNITS):
+            load_x(i)
+            if i == 1:
+                for quadrant in range(QUADRANTS):
+                    rows = slice(SCALE_ROWS * quadrant, SCALE_ROWS * (quadrant + 1))
+                    nc.sync.dma_start(
+                        out=w_scales[32 * quadrant : 32 * quadrant + SCALE_ROWS].bitcast(I32),
+                        in_=Wq_scales[:, rows, :].rearrange("g r n -> r g n").bitcast(I32),
+                    )
+            if i in W_AFTER:
+                load_w(W_AFTER.index(i))
+            if i == G_LOAD:
                 nc.sync.dma_start(out=kv_sb[:], in_=kv.rearrange("b o l k -> l (b o) k"))
                 nc.sync.dma_start(out=d_sb[:], in_=decay_mask[0])
                 nc.sync.dma_start(out=bias_rows[0:1, :], in_=bq.unsqueeze(0))
-        for i in range(UNITS_PER_SAMPLE + 2, UNITS):
-            load_x(i)
 
         one = const.tile([P, 1], F32)
         nc.vector.memset(one[:], 1.0)
@@ -155,62 +158,57 @@ def tile_parallelretention_pb_k_kernel(tc, x, Wq_words, Wq_scales, bq, kv, decay
             sorted_words = sorted_pool.tile([P, SORTED_PASSES, PAIRS, P], F32)
             nc.vector.tensor_copy(
                 out=sorted_words[:],
-                in_=x_words[:, 0 : SORTED_PASSES * WORDS_PER_PASS].rearrange(
+                in_=x_words[:, FIRST_SORTED * WORDS_PER_PASS : UNIT_PASSES * WORDS_PER_PASS].rearrange(
                     "r (g p u) -> r g u p", g=SORTED_PASSES, u=PAIRS
                 ),
             )
             x_sorted[i] = sorted_words
 
         def words_of_pass(i, g, u):
-            if i in x_sorted and g < SORTED_PASSES:
-                return x_sorted[i][:, g, u, :]
+            if i in x_sorted and g >= FIRST_SORTED:
+                return x_sorted[i][:, g - FIRST_SORTED, u, :]
             part, g_in_part = divmod(g, UNIT_PASSES // len(x_parts[i]))
             x_words = x_parts[i][part][:].bitcast(F32)
             return x_words[:, g_in_part * WORDS_PER_PASS + u : (g_in_part + 1) * WORDS_PER_PASS : PAIRS]
 
-        def transpose_and_quantise(i):
-            if i + 1 < UNITS and not is_edge(i + 1):
-                sort_words(i + 1)
+        x_grouped = {}
+        transposed = {}
+
+        def transpose(i):
             grouped = grouped_pool.tile([P, UNIT_PASSES * TOKENS * PACK], BF16, align_bytes=64)
-            grouped_words = grouped[:].bitcast(F32).rearrange("p (g r u) -> p g r u", g=UNIT_PASSES, u=PAIRS)
             codes = codes_pool.tile([P, UNIT_PASSES * TOKENS], U32, align_bytes=64)
             scales = codes_pool.tile([P, UNIT_PASSES * TOKENS], U8, align_bytes=64)
+            x_grouped[i] = grouped
             x_codes[i] = codes
             x_scales[i] = scales
-
-            def quantise(first_bank, banks):
-                cols = slice(first_bank * BANK_COLS, (first_bank + banks) * BANK_COLS)
-                nc.vector.quantize_mx(
-                    out=codes[:, cols].bitcast(FP8X4),
-                    scales=scales[:, cols],
-                    in_=grouped[:, first_bank * BANK_COLS * PACK : (first_bank + banks) * BANK_COLS * PACK],
-                )
-
-            vector_banks = (1, 3) if is_edge(i) else (2,) if i % 2 == 1 else ()
             for j in range(UNIT_BANKS):
                 xt_ps = psum_xt.tile([P, BANK_PASSES, PAIRS, TOKENS], F32, tag="xt")
                 for g in range(BANK_PASSES):
                     for u in range(PAIRS):
                         nc.tensor.transpose(xt_ps[:, g, u, :], words_of_pass(i, j * BANK_PASSES + g, u), ident_f32[:])
-                copy = nc.vector.tensor_copy if j in vector_banks else nc.scalar.copy
-                copy(
-                    out=grouped_words[:, j * BANK_PASSES : (j + 1) * BANK_PASSES, :, :],
-                    in_=xt_ps[:].rearrange("p g u r -> p g r u"),
-                )
-                if is_edge(i):
-                    if j >= 1:
-                        quantise(j - 1, 1)
-                    if j == UNIT_BANKS - 1:
-                        quantise(j, 1)
-                elif j == 2:
-                    quantise(0, 2)
-                elif j == 3:
-                    quantise(2, 2)
+                transposed[i, j] = xt_ps
+                if j not in vector_banks(i):
+                    copy_out(i, j, nc.scalar.copy)
+
+        def copy_out(i, j, copy):
+            grouped_words = x_grouped[i][:].bitcast(F32).rearrange("p (g r u) -> p g r u", g=UNIT_PASSES, u=PAIRS)
+            copy(
+                out=grouped_words[:, j * BANK_PASSES : (j + 1) * BANK_PASSES, :, :],
+                in_=transposed[i, j][:].rearrange("p g u r -> p g r u"),
+            )
+
+        def quantise(i, first_bank, banks):
+            cols = slice(first_bank * BANK_COLS, (first_bank + banks) * BANK_COLS)
+            nc.vector.quantize_mx(
+                out=x_codes[i][:, cols].bitcast(FP8X4),
+                scales=x_scales[i][:, cols],
+                in_=x_grouped[i][:, first_bank * BANK_COLS * PACK : (first_bank + banks) * BANK_COLS * PACK],
+            )
 
         def multiply(i):
-            b, c = divmod(i, UNITS_PER_SAMPLE)
+            b, c = ORDER[i]
             if c == 0:
-                qT_ps = psum_q.tile([P, TOKENS], F32)
+                qT_ps = psum_q.tile([P, TOKENS], F32, tag="q")
                 qT[b] = qT_ps
             for g in range(UNIT_PASSES):
                 w_pass = c * UNIT_PASSES + g
@@ -241,7 +239,7 @@ def tile_parallelretention_pb_k_kernel(tc, x, Wq_words, Wq_scales, bq, kv, decay
             norm[b, "row_sum"] = row_sum
 
         def centre(b):
-            norm_ps = psum_norm.tile([P, FEATURES + 4], F32)
+            norm_ps = psum_q.tile([P, FEATURES + 4], F32, tag="q")
             mean_ps = norm_ps[:, MEAN_COL : MEAN_COL + 1]
             nc.tensor.matmul(out=mean_ps, lhsT=mean_weights[:], rhs=norm[b, "row_sum"][:], start=True, stop=True)
             nc.tensor.transpose(norm_ps[:, 0:FEATURES], norm[b, "yT"][:], ident_f32[:])
@@ -279,29 +277,50 @@ def tile_parallelretention_pb_k_kernel(tc, x, Wq_words, Wq_scales, bq, kv, decay
             )
             nc.sync.dma_start(out=out[b], in_=result[:])
 
-        def sample_that_ended(i):
-            return i // UNITS_PER_SAMPLE if 0 <= i < UNITS and i % UNITS_PER_SAMPLE == UNITS_PER_SAMPLE - 1 else None
+        ends = {i: b for i, (b, c) in enumerate(ORDER) if c == UNITS_PER_SAMPLE - 1}
+
+        def vector_banks(i):
+            return (1,) if is_edge(i) else ()
 
         last = UNITS - 1
         for i in range(UNITS):
-            if i == last:
-                multiply(i - 2)
-            transpose_and_quantise(i)
-            if i == UNITS_PER_SAMPLE:
+            if i - 3 in ends:
+                product(ends[i - 3])
+            if i - 4 in ends:
+                centre(ends[i - 4])
+            if i - 5 in ends:
+                scale_and_store(ends[i - 5])
+            transpose(i)
+            if i >= 1:
+                quantise(i - 1, 0, 2)
+            if i < last:
+                for j in vector_banks(i):
+                    copy_out(i, j, nc.vector.tensor_copy)
+                if not is_edge(i + 1):
+                    sort_words(i + 1)
+            if i >= 1:
+                quantise(i - 1, 2, 2)
+            if i == G_LOAD + 1:
                 transpose_small_inputs()
-            if sample_that_ended(i - 4) is not None:
-                scale_and_store(sample_that_ended(i - 4))
-            if sample_that_ended(i - 3) is not None:
-                centre(sample_that_ended(i - 3))
-            if i == last:
-                multiply(i - 1)
-                multiply(i)
-            elif i >= 2:
-                multiply(i - 2)
-            if i == UNITS_PER_SAMPLE:
+            if i == G_LOAD + 2:
                 multiply_g()
-            if sample_that_ended(i - 2) is not None:
-                product(sample_that_ended(i - 2))
-        product(SAMPLES - 1)
-        centre(SAMPLES - 1)
-        scale_and_store(SAMPLES - 1)
+            if i >= 2:
+                multiply(i - 2)
+        multiply(last - 1)
+        for j in range(UNIT_BANKS):
+            if j in vector_banks(last):
+                copy_out(last, j, nc.vector.tensor_copy)
+            quantise(last, j, 1)
+        if last - 4 in ends:
+            scale_and_store(ends[last - 4])
+        elif last - 3 in ends:
+            centre(ends[last - 3])
+            scale_and_store(ends[last - 3])
+        multiply(last)
+        tail = [ends[i] for i in (last - 2, last - 1, last) if i in ends]
+        for b in tail:
+            product(b)
+        for b in tail:
+            centre(b)
+        for b in tail:
+            scale_and_store(b)

@@ -31,14 +31,14 @@ UNIT_BANKS = UNIT_PASSES // BANK_PASSES
 UNIT_K = UNIT_PASSES * K_PASS
 UNITS_PER_SAMPLE = PASSES // UNIT_PASSES
 UNITS = SAMPLES * UNITS_PER_SAMPLE
-ORDER = [(b, c) for b in range(SAMPLES) for c in range(UNITS_PER_SAMPLE)]
+ORDER = [(b, c) for c in range(UNITS_PER_SAMPLE) for b in range(2)] + [(b, c) for b in range(2, SAMPLES) for c in range(UNITS_PER_SAMPLE)]
 BANK_COLS = BANK_PASSES * TOKENS
 SORTED_PASSES = 6
 
 FIRST_SORTED = UNIT_PASSES - SORTED_PASSES
 
-W_AFTER = (1, 2, 3, 4)
-G_LOAD = 3
+W_AFTER = (2, 4, 6, 8)
+G_LOAD = 5
 
 SCALE_ROWS = 4
 QUADRANTS = 4
@@ -59,8 +59,8 @@ def tile_parallelretention_pb_k_kernel(tc, x, Wq_words, Wq_scales, bq, kv, decay
         grouped_pool = ctx.enter_context(tc.tile_pool(name="grouped", bufs=3))
         codes_pool = ctx.enter_context(tc.tile_pool(name="codes", bufs=4))
         norm_pool = ctx.enter_context(tc.tile_pool(name="norm", bufs=2))
-        psum_xt = ctx.enter_context(tc.psum_pool(name="psum_xt", bufs=6))
-        psum_q = ctx.enter_context(tc.psum_pool(name="psum_q", bufs=2))
+        psum_xt = ctx.enter_context(tc.psum_pool(name="psum_xt", bufs=5))
+        psum_q = ctx.enter_context(tc.psum_pool(name="psum_q", bufs=3))
         ctx.enter_context(tc.manual_schedule())
 
         ident_f32 = const.tile([P, P], F32)
@@ -104,7 +104,7 @@ def tile_parallelretention_pb_k_kernel(tc, x, Wq_words, Wq_scales, bq, kv, decay
 
         for i in range(UNITS):
             load_x(i)
-            if i == 1:
+            if i == 2:
                 for quadrant in range(QUADRANTS):
                     rows = slice(SCALE_ROWS * quadrant, SCALE_ROWS * (quadrant + 1))
                     nc.sync.dma_start(
@@ -280,7 +280,7 @@ def tile_parallelretention_pb_k_kernel(tc, x, Wq_words, Wq_scales, bq, kv, decay
         ends = {i: b for i, (b, c) in enumerate(ORDER) if c == UNITS_PER_SAMPLE - 1}
 
         def vector_banks(i):
-            return (1,) if is_edge(i) else ()
+            return ()
 
         last = UNITS - 1
         for i in range(UNITS):

@@ -53,7 +53,7 @@ def tile_parallelretention_pb_k_kernel(tc, x, Wq_words, Wq_scales, bq, kv, decay
     nc = tc.nc
     with ExitStack() as ctx:
         const = ctx.enter_context(tc.tile_pool(name="const", bufs=1))
-        x_pool = ctx.enter_context(tc.tile_pool(name="x", bufs=UNITS - 2))
+        x_pool = ctx.enter_context(tc.tile_pool(name="x", bufs=UNITS))
         x_edge_pool = ctx.enter_context(tc.tile_pool(name="x_edge", bufs=4))
         sorted_pool = ctx.enter_context(tc.tile_pool(name="sorted", bufs=3))
         grouped_pool = ctx.enter_context(tc.tile_pool(name="grouped", bufs=3))
@@ -79,14 +79,14 @@ def tile_parallelretention_pb_k_kernel(tc, x, Wq_words, Wq_scales, bq, kv, decay
         d_sb = const.tile([P, P], BF16)
 
         def is_edge(i):
-            return i == 0 or i == UNITS - 1
+            return i == 0
 
         x_parts = {}
 
         def load_x(i):
             b, c = ORDER[i]
-            parts = 2 if is_edge(i) else 1
-            pool = x_edge_pool if is_edge(i) else x_pool
+            parts = 1
+            pool = x_pool
             x_parts[i] = []
             for h in range(parts):
                 width = UNIT_K // parts
@@ -291,13 +291,10 @@ def tile_parallelretention_pb_k_kernel(tc, x, Wq_words, Wq_scales, bq, kv, decay
             if i - 5 in ends:
                 scale_and_store(ends[i - 5])
             transpose(i)
+            if i < last and not is_edge(i + 1):
+                sort_words(i + 1)
             if i >= 1:
                 quantise(i - 1, 0, 2)
-            if i < last:
-                for j in vector_banks(i):
-                    copy_out(i, j, nc.vector.tensor_copy)
-                if not is_edge(i + 1):
-                    sort_words(i + 1)
             if i >= 1:
                 quantise(i - 1, 2, 2)
             if i == G_LOAD + 1:

from contextlib import ExitStack

import concourse.mybir as mybir
from concourse.masks import make_identity

F32 = mybir.dt.float32
BF16 = mybir.dt.bfloat16
I32 = mybir.dt.int32
U32 = mybir.dt.uint32
U8 = mybir.dt.uint8
FP8X4 = mybir.dt.float8_e4m3fn_x4
ALU = mybir.AluOpType
ACT = mybir.ActivationFunctionType

P = 128
SAMPLES = 4
TOKENS = 128
FEATURES = 128
K_TOTAL = 16384
EPS = 1e-5

PACK = 4
K_PASS = P * PACK
PASSES = K_TOTAL // K_PASS
PAIRS = 2
WORDS_PER_PASS = P * PAIRS

BANK_PASSES = 2
UNIT_PASSES = 8
UNIT_BANKS = UNIT_PASSES // BANK_PASSES
UNIT_K = UNIT_PASSES * K_PASS
UNITS_PER_SAMPLE = PASSES // UNIT_PASSES
UNITS = SAMPLES * UNITS_PER_SAMPLE
ORDER = [(b, c) for c in range(UNITS_PER_SAMPLE) for b in range(2)] + [(b, c) for b in range(2, SAMPLES) for c in range(UNITS_PER_SAMPLE)]
BANK_COLS = BANK_PASSES * TOKENS
SORTED_PASSES = 6

FIRST_SORTED = UNIT_PASSES - SORTED_PASSES

W_AFTER = (2, 4, 6, 8)
G_LOAD = 5

SCALE_ROWS = 4
QUADRANTS = 4

MEAN_COL = FEATURES
VAR_COL = FEATURES + 2

FLOPS = 2 * SAMPLES * TOKENS * FEATURES * (K_TOTAL + P)


def tile_parallelretention_pb_k_kernel(tc, x, Wq_words, Wq_scales, bq, kv, decay_mask, out):
    nc = tc.nc
    with ExitStack() as ctx:
        const = ctx.enter_context(tc.tile_pool(name="const", bufs=1))
        x_pool = ctx.enter_context(tc.tile_pool(name="x", bufs=UNITS))
        x_edge_pool = ctx.enter_context(tc.tile_pool(name="x_edge", bufs=4))
        sorted_pool = ctx.enter_context(tc.tile_pool(name="sorted", bufs=3))
        grouped_pool = ctx.enter_context(tc.tile_pool(name="grouped", bufs=3))
        codes_pool = ctx.enter_context(tc.tile_pool(name="codes", bufs=4))
        norm_pool = ctx.enter_context(tc.tile_pool(name="norm", bufs=2))
        psum_xt = ctx.enter_context(tc.psum_pool(name="psum_xt", bufs=5))
        psum_q = ctx.enter_context(tc.psum_pool(name="psum_q", bufs=3))
        ctx.enter_context(tc.manual_schedule())

        ident_f32 = const.tile([P, P], F32)
        make_identity(nc, ident_f32[:])
        ident_bf16 = const.tile([P, P], BF16)
        make_identity(nc, ident_bf16[:])
        mean_weights = const.tile([P, P], F32)
        nc.gpsimd.memset(mean_weights[:], 1.0 / (TOKENS * FEATURES))

        w_codes = const.tile([P, PASSES, FEATURES], U32, align_bytes=64)
        w_scales = const.tile([P, PASSES, FEATURES], U8, align_bytes=64)
        nc.vector.memset(w_scales[:].bitcast(I32), 0)
        bias_rows = const.tile([P, FEATURES], BF16)
        nc.vector.memset(bias_rows[:].bitcast(I32), 0)
        kv_sb = const.tile([P, SAMPLES, P], BF16)
        d_sb = const.tile([P, P], BF16)

        def is_edge(i):
            return i == 0

        x_parts = {}

        def load_x(i):
            b, c = ORDER[i]
            parts = 1
            pool = x_pool
            x_parts[i] = []
            for h in range(parts):
                width = UNIT_K // parts
                x_t = pool.tile([P, width], BF16, name="x_t")
                first = c * UNIT_K + h * width
                nc.sync.dma_start(out=x_t[:], in_=x[b, 0, :, first : first + width])
                x_parts[i].append(x_t)

        def load_w(c):
            passes = slice(c * UNIT_PASSES, (c + 1) * UNIT_PASSES)
            nc.sync.dma_start(
                out=w_codes[:, passes, :].bitcast(I32),
                in_=Wq_words[passes].rearrange("g p n t -> p g (n t)").bitcast(I32),
            )

        for i in range(UNITS):
            load_x(i)
            if i == 2:
                for quadrant in range(QUADRANTS):
                    rows = slice(SCALE_ROWS * quadrant, SCALE_ROWS * (quadrant + 1))
                    nc.sync.dma_start(
                        out=w_scales[32 * quadrant : 32 * quadrant + SCALE_ROWS].bitcast(I32),
                        in_=Wq_scales[:, rows, :].rearrange("g r n -> r g n").bitcast(I32),
                    )
            if i in W_AFTER:
                load_w(W_AFTER.index(i))
            if i == G_LOAD:
                nc.sync.dma_start(out=kv_sb[:], in_=kv.rearrange("b o l k -> l (b o) k"))
                nc.sync.dma_start(out=d_sb[:], in_=decay_mask[0])
                nc.sync.dma_start(out=bias_rows[0:1, :], in_=bq.unsqueeze(0))

        one = const.tile([P, 1], F32)
        nc.vector.memset(one[:], 1.0)
        warm = const.tile([P, 1], F32)
        nc.scalar.activation(out=warm[:], in_=one[:], func=ACT.Abs_reciprocal_sqrt)

        kvT_dT = const.tile([P, SAMPLES + 1, P], BF16)
        bias_col = const.tile([P, 1], F32)
        gT = const.tile([P, SAMPLES * TOKENS], F32)

        def transpose_small_inputs():
            small_ps = psum_xt.tile([P, SAMPLES + 2, P], BF16, tag="xt")
            for b in range(SAMPLES):
                nc.tensor.transpose(small_ps[:, b, :], kv_sb[:, b, :], ident_bf16[:])
            nc.tensor.transpose(small_ps[:, SAMPLES, :], d_sb[:], ident_bf16[:])
            nc.tensor.transpose(small_ps[:, SAMPLES + 1, :], bias_rows[:], ident_bf16[:])
            nc.vector.tensor_copy(out=kvT_dT[:], in_=small_ps[:, 0 : SAMPLES + 1, :])
            nc.vector.tensor_copy(out=bias_col[:], in_=small_ps[:, SAMPLES + 1, 0:1])

        def multiply_g():
            gT_ps = psum_xt.tile([P, SAMPLES * TOKENS], F32, tag="xt")
            nc.tensor.matmul(
                out=gT_ps[:],
                lhsT=kvT_dT[:, SAMPLES, :],
                rhs=kvT_dT[:, 0:SAMPLES, :].rearrange("k b l -> k (b l)"),
                start=True,
                stop=True,
            )
            nc.scalar.copy(out=gT[:], in_=gT_ps[:])

        x_sorted = {}
        x_codes = {}
        x_scales = {}
        qT = {}
        norm = {}

        def sort_words(i):
            x_words = x_parts[i][0][:].bitcast(F32)
            sorted_words = sorted_pool.tile([P, SORTED_PASSES, PAIRS, P], F32)
            nc.vector.tensor_copy(
                out=sorted_words[:],
                in_=x_words[:, FIRST_SORTED * WORDS_PER_PASS : UNIT_PASSES * WORDS_PER_PASS].rearrange(
                    "r (g p u) -> r g u p", g=SORTED_PASSES, u=PAIRS
                ),
            )
            x_sorted[i] = sorted_words

        def words_of_pass(i, g, u):
            if i in x_sorted and g >= FIRST_SORTED:
                return x_sorted[i][:, g - FIRST_SORTED, u, :]
            part, g_in_part = divmod(g, UNIT_PASSES // len(x_parts[i]))
            x_words = x_parts[i][part][:].bitcast(F32)
            return x_words[:, g_in_part * WORDS_PER_PASS + u : (g_in_part + 1) * WORDS_PER_PASS : PAIRS]

        x_grouped = {}
        transposed = {}

        def transpose(i):
            grouped = grouped_pool.tile([P, UNIT_PASSES * TOKENS * PACK], BF16, align_bytes=64)
            codes = codes_pool.tile([P, UNIT_PASSES * TOKENS], U32, align_bytes=64)
            scales = codes_pool.tile([P, UNIT_PASSES * TOKENS], U8, align_bytes=64)
            x_grouped[i] = grouped
            x_codes[i] = codes
            x_scales[i] = scales
            for j in range(UNIT_BANKS):
                xt_ps = psum_xt.tile([P, BANK_PASSES, PAIRS, TOKENS], F32, tag="xt")
                for g in range(BANK_PASSES):
                    for u in range(PAIRS):
                        nc.tensor.transpose(xt_ps[:, g, u, :], words_of_pass(i, j * BANK_PASSES + g, u), ident_f32[:])
                transposed[i, j] = xt_ps
                if j not in vector_banks(i):
                    copy_out(i, j, nc.scalar.copy)

        def copy_out(i, j, copy):
            grouped_words = x_grouped[i][:].bitcast(F32).rearrange("p (g r u) -> p g r u", g=UNIT_PASSES, u=PAIRS)
            copy(
                out=grouped_words[:, j * BANK_PASSES : (j + 1) * BANK_PASSES, :, :],
                in_=transposed[i, j][:].rearrange("p g u r -> p g r u"),
            )

        def quantise(i, first_bank, banks):
            cols = slice(first_bank * BANK_COLS, (first_bank + banks) * BANK_COLS)
            nc.vector.quantize_mx(
                out=x_codes[i][:, cols].bitcast(FP8X4),
                scales=x_scales[i][:, cols],
                in_=x_grouped[i][:, first_bank * BANK_COLS * PACK : (first_bank + banks) * BANK_COLS * PACK],
            )

        def multiply(i):
            b, c = ORDER[i]
            if c == 0:
                qT_ps = psum_q.tile([P, TOKENS], F32, tag="q")
                qT[b] = qT_ps
            for g in range(UNIT_PASSES):
                w_pass = c * UNIT_PASSES + g
                cols = slice(g * TOKENS, (g + 1) * TOKENS)
                nc.tensor.matmul_mx(
                    out=qT[b][:],
                    lhsT=w_codes[:, w_pass, :].bitcast(FP8X4),
                    lhsT_scale=w_scales[:, w_pass, :],
                    rhs=x_codes[i][:, cols].bitcast(FP8X4),
                    rhs_scale=x_scales[i][:, cols],
                    start=(w_pass == 0),
                    stop=(w_pass == PASSES - 1),
                )

        def product(b):
            yT = norm_pool.tile([P, TOKENS], F32)
            row_sum = norm_pool.tile([P, 1], F32)
            nc.vector.scalar_tensor_tensor(
                out=yT[:],
                in0=qT[b][:],
                scalar=bias_col[:, 0:1],
                in1=gT[:, b * TOKENS : (b + 1) * TOKENS],
                op0=ALU.add,
                op1=ALU.mult,
                accum_out=row_sum[:],
            )
            norm[b, "yT"] = yT
            norm[b, "row_sum"] = row_sum

        def centre(b):
            norm_ps = psum_q.tile([P, FEATURES + 4], F32, tag="q")
            mean_ps = norm_ps[:, MEAN_COL : MEAN_COL + 1]
            nc.tensor.matmul(out=mean_ps, lhsT=mean_weights[:], rhs=norm[b, "row_sum"][:], start=True, stop=True)
            nc.tensor.transpose(norm_ps[:, 0:FEATURES], norm[b, "yT"][:], ident_f32[:])
            products = norm_pool.tile([P, TOKENS], F32)
            row_squares = norm_pool.tile([P, 1], F32)
            nc.vector.scalar_tensor_tensor(
                out=products[:],
                in0=norm[b, "yT"][:],
                scalar=mean_ps,
                in1=norm[b, "yT"][:],
                op0=ALU.subtract,
                op1=ALU.mult,
                accum_out=row_squares[:],
            )
            mean = norm_pool.tile([P, 1], F32)
            nc.vector.tensor_copy(out=mean[:], in_=mean_ps)
            norm[b, "ps"] = norm_ps
            norm[b, "mean"] = mean
            norm[b, "row_squares"] = row_squares

        def scale_and_store(b):
            norm_ps = norm[b, "ps"]
            var_ps = norm_ps[:, VAR_COL : VAR_COL + 1]
            nc.tensor.matmul(out=var_ps, lhsT=mean_weights[:], rhs=norm[b, "row_squares"][:], start=True, stop=True)
            rstd = norm_pool.tile([P, 1], F32)
            nc.scalar.activation(out=rstd[:], in_=var_ps, func=ACT.Abs_reciprocal_sqrt, bias=EPS)
            result = norm_pool.tile([P, FEATURES], F32)
            nc.vector.tensor_scalar(
                out=result[:],
                in0=norm_ps[:, 0:FEATURES],
                scalar1=norm[b, "mean"][:, 0:1],
                scalar2=rstd[:, 0:1],
                op0=ALU.subtract,
                op1=ALU.mult,
            )
            nc.sync.dma_start(out=out[b], in_=result[:])

        ends = {i: b for i, (b, c) in enumerate(ORDER) if c == UNITS_PER_SAMPLE - 1}

        def vector_banks(i):
            return ()

        last = UNITS - 1
        for i in range(UNITS):
            if i - 3 in ends:
                product(ends[i - 3])
            if i - 4 in ends:
                centre(ends[i - 4])
            if i - 5 in ends:
                scale_and_store(ends[i - 5])
            transpose(i)
            if i < last and not is_edge(i + 1):
                sort_words(i + 1)
            if i >= 1:
                quantise(i - 1, 0, 2)
            if i >= 1:
                quantise(i - 1, 2, 2)
            if i == G_LOAD + 1:
                transpose_small_inputs()
            if i == G_LOAD + 2:
                multiply_g()
            if i >= 2:
                multiply(i - 2)
        multiply(last - 1)
        for j in range(UNIT_BANKS):
            if j in vector_banks(last):
                copy_out(last, j, nc.vector.tensor_copy)
            quantise(last, j, 1)
        if last - 4 in ends:
            scale_and_store(ends[last - 4])
        elif last - 3 in ends:
            centre(ends[last - 3])
            scale_and_store(ends[last - 3])
        multiply(last)
        tail = [ends[i] for i in (last - 2, last - 1, last) if i in ends]
        for b in tail:
            product(b)
        for b in tail:
            centre(b)
        for b in tail:
            scale_and_store(b)
